import numpy as np
import ml_dtypes

BF16 = ml_dtypes.bfloat16


def bf(x):
    return np.asarray(x, np.float32).astype(BF16)


def f32(x):
    return np.asarray(x, np.float32)


def f64(x):
    return np.asarray(x).astype(np.float64)


def striped(idx):
    return np.tile(idx.reshape(-1, 16).T, (8, 1))


B, R, C, S, N = 256, 16, 256, 2048, 2048
ENTROPY_REG = 0.1
DIAG_PENALTY = 100000.0


def setup_inputs():
    latent = f32(5.0 * np.random.standard_normal((B, C)))
    edges = f32(np.where(np.random.uniform(size=(C, S)) < 0.05, 0.5, 0.0))
    query = f32(np.where(np.random.uniform(size=(B, N)) < 0.1, 1.0, -1.0))
    idx = np.random.permutation(np.tile(np.arange(S), 2))[:N]
    return {"latent": latent, "edges": edges, "query": query, "offs": striped(idx)}


def reference(latent, edges, query, offs):
    idx = offs[:16].T.reshape(-1)
    cost = -ENTROPY_REG * f64(latent).reshape(B, R, R) - DIAG_PENALTY * np.eye(R)
    e = np.exp(cost - cost.max(axis=-1, keepdims=True))
    adj = e / e.sum(axis=-1, keepdims=True)
    img = adj.reshape(B, C) @ f64(edges)[:, idx]
    img = 2.0 * (img - 0.5)
    return np.where(f64(query) == 1.0, 1.0, img)

@@ -1,0 +1,141 @@
+import concourse.mybir as mybir
+from concourse.masks import make_identity
+
+F32 = mybir.dt.float32
+BF16 = mybir.dt.bfloat16
+U16 = mybir.dt.uint16
+ALU = mybir.AluOpType
+ACT = mybir.ActivationFunctionType
+AXIS = mybir.AxisListType
+
+P = 128
+B, R, C, S, N = 256, 16, 256, 2048, 2048
+SAMPLE_BLOCKS = B // P
+PAIR_BLOCKS = C // P
+PIECE = 512
+PIECES = N // PIECE
+ENTROPY_REG = 0.1
+DIAG_PENALTY = 100000.0
+
+FLOPS = 2 * B * C * N
+
+
+def tile_inferencemodel_kernel(tc, latent, edges, query, offs, out):
+    nc = tc.nc
+    with (
+        tc.tile_pool(name="held", bufs=1) as held,
+        tc.psum_pool(name="flip", bufs=1) as flip,
+        tc.psum_pool(name="banks", bufs=6) as banks,
+    ):
+        offsets = held.tile([P, N // 16], U16, name="offsets")
+        nc.sync.dma_start(offsets[:], offs)
+        lat = held.tile([P, SAMPLE_BLOCKS * C], F32, name="lat")
+        nc.sync.dma_start(
+            lat[:].rearrange("p (h c) -> p h c", h=SAMPLE_BLOCKS),
+            latent.rearrange("(h p) c -> p h c", p=P),
+        )
+        windows = []
+        for cb in range(PAIR_BLOCKS):
+            window = held.tile([P, S], F32, name=f"window{cb}")
+            nc.sync.dma_start(window[:], edges[cb * P : (cb + 1) * P, :])
+            windows.append(window)
+        query_view = query.rearrange("(h p) n -> p h n", p=P)
+        out_view = out.rearrange("(h p) n -> p h n", p=P)
+        asked = []
+        for piece in range(PIECES):
+            asked_piece = held.tile([P, SAMPLE_BLOCKS, PIECE], F32, name=f"asked{piece}")
+            nc.sync.dma_start(asked_piece[:], query_view[:, :, piece * PIECE : (piece + 1) * PIECE])
+            asked.append(asked_piece)
+
+        penalty = held.tile([P, SAMPLE_BLOCKS * C], F32, name="penalty")
+        nc.vector.memset(penalty[:], 0.0)
+        nc.gpsimd.affine_select(
+            out=penalty[:],
+            in_=penalty[:],
+            pattern=[[0, SAMPLE_BLOCKS], [1, R], [-1, R]],
+            compare_op=ALU.not_equal,
+            fill=-DIAG_PENALTY,
+            base=0,
+            channel_multiplier=0,
+        )
+        identity = held.tile([P, P], BF16, name="identity")
+        make_identity(nc, identity[:])
+
+        groups = SAMPLE_BLOCKS * R
+
+        def grouped(tile_ap):
+            return tile_ap.rearrange("p (g k) -> p g k", k=R)
+
+        def per_group(tile_ap):
+            return tile_ap.unsqueeze(2).to_broadcast([P, groups, R])
+
+        cost = held.tile([P, SAMPLE_BLOCKS * C], F32, name="cost")
+        nc.vector.scalar_tensor_tensor(
+            out=cost[:], in0=lat[:], scalar=-ENTROPY_REG, in1=penalty[:], op0=ALU.mult, op1=ALU.add
+        )
+        top = held.tile([P, groups], F32, name="top")
+        nc.vector.tensor_reduce(out=top[:], in_=grouped(cost[:]), axis=AXIS.X, op=ALU.max)
+        shifted = held.tile([P, SAMPLE_BLOCKS * C], F32, name="shifted")
+        nc.vector.tensor_tensor(grouped(shifted[:]), grouped(cost[:]), per_group(top[:]), ALU.subtract)
+        expd = held.tile([P, SAMPLE_BLOCKS * C], F32, name="expd")
+        nc.scalar.activation(expd[:], shifted[:], ACT.Exp)
+        total = held.tile([P, groups], F32, name="total")
+        nc.vector.tensor_reduce(out=total[:], in_=grouped(expd[:]), axis=AXIS.X, op=ALU.add)
+        inverse = held.tile([P, groups], F32, name="inverse")
+        nc.vector.reciprocal(inverse[:], total[:])
+        twice_adj = held.tile([P, SAMPLE_BLOCKS * C], BF16, name="twice_adj")
+        nc.vector.scalar_tensor_tensor(
+            out=grouped(twice_adj[:]),
+            in0=grouped(expd[:]),
+            scalar=2.0,
+            in1=per_group(inverse[:]),
+            op0=ALU.mult,
+            op1=ALU.mult,
+        )
+
+        flipped = flip.tile([P, PAIR_BLOCKS * SAMPLE_BLOCKS * P], BF16, name="flipped")
+        for cb in range(PAIR_BLOCKS):
+            for h in range(SAMPLE_BLOCKS):
+                block = cb * SAMPLE_BLOCKS + h
+                nc.tensor.transpose(
+                    flipped[:, block * P : (block + 1) * P],
+                    twice_adj[:, h * C + cb * P : h * C + (cb + 1) * P],
+                    identity[:],
+                )
+        weights = held.tile([P, PAIR_BLOCKS * SAMPLE_BLOCKS * P], F32, name="weights")
+        nc.vector.tensor_copy(weights[:], flipped[:])
+
+        keep = []
+        for piece in range(PIECES):
+            keep_piece = held.tile([P, SAMPLE_BLOCKS, PIECE], F32, name=f"keep{piece}")
+            nc.vector.tensor_scalar(
+                out=keep_piece[:], in0=asked[piece][:], scalar1=1.0, scalar2=None, op0=ALU.not_equal
+            )
+            keep.append(keep_piece)
+
+        for piece in range(PIECES):
+            listed = offsets[:, piece * (PIECE // 16) : (piece + 1) * (PIECE // 16)]
+            picked = []
+            for cb in range(PAIR_BLOCKS):
+                columns = held.tile([P, PIECE], F32, name=f"picked{cb}_{piece}")
+                nc.scalar.activation(columns[:], windows[cb][:].indirect(listed), ACT.Copy)
+                picked.append(columns)
+            result = held.tile([P, SAMPLE_BLOCKS, PIECE], F32, name=f"result{piece}")
+            for h in range(SAMPLE_BLOCKS):
+                bank = banks.tile([P, PIECE], F32, name="bank")
+                for cb in range(PAIR_BLOCKS):
+                    block = cb * SAMPLE_BLOCKS + h
+                    nc.tensor.matmul(
+                        bank[:],
+                        weights[:, block * P : (block + 1) * P],
+                        picked[cb][:],
+                        start=(cb == 0),
+                        stop=(cb == PAIR_BLOCKS - 1),
+                    )
+                nc.vector.scalar_tensor_tensor(
+                    out=result[:, h, :], in0=bank[:], scalar=-2.0, in1=keep[piece][:, h, :], op0=ALU.add, op1=ALU.mult
+                )
+                nc.vector.tensor_scalar(
+                    out=result[:, h, :], in0=result[:, h, :], scalar1=1.0, scalar2=None, op0=ALU.add
+                )
+            nc.sync.dma_start(out_view[:, :, piece * PIECE : (piece + 1) * PIECE], result[:])

@@ -20,20 +20,29 @@ DIAG_PENALTY = 100000.0
 FLOPS = 2 * B * C * N
 
 
+def grouped(tile_ap):
+    return tile_ap.rearrange("p (i k) -> p i k", k=R)
+
+
+def per_row(tile_ap):
+    return tile_ap.unsqueeze(2).to_broadcast([P, R, R])
+
+
 def tile_inferencemodel_kernel(tc, latent, edges, query, offs, out):
     nc = tc.nc
     with (
         tc.tile_pool(name="held", bufs=1) as held,
-        tc.psum_pool(name="flip", bufs=1) as flip,
-        tc.psum_pool(name="banks", bufs=6) as banks,
+        tc.tile_pool(name="ring", bufs=2) as ring,
+        tc.psum_pool(name="flip", bufs=SAMPLE_BLOCKS) as flip,
+        tc.psum_pool(name="banks", bufs=3) as banks,
     ):
+        lat = []
+        for h in range(SAMPLE_BLOCKS):
+            lat_h = held.tile([P, C], F32, name=f"lat{h}")
+            nc.sync.dma_start(lat_h[:], latent[h * P : (h + 1) * P, :])
+            lat.append(lat_h)
         offsets = held.tile([P, N // 16], U16, name="offsets")
         nc.sync.dma_start(offsets[:], offs)
-        lat = held.tile([P, SAMPLE_BLOCKS * C], F32, name="lat")
-        nc.sync.dma_start(
-            lat[:].rearrange("p (h c) -> p h c", h=SAMPLE_BLOCKS),
-            latent.rearrange("(h p) c -> p h c", p=P),
-        )
         windows = []
         for cb in range(PAIR_BLOCKS):
             window = held.tile([P, S], F32, name=f"window{cb}")
@@ -47,12 +56,15 @@ def tile_inferencemodel_kernel(tc, latent, edges, query, offs, out):
             nc.sync.dma_start(asked_piece[:], query_view[:, :, piece * PIECE : (piece + 1) * PIECE])
             asked.append(asked_piece)
 
-        penalty = held.tile([P, SAMPLE_BLOCKS * C], F32, name="penalty")
+        warm = held.tile([P, 1], F32, name="warm")
+        nc.vector.memset(warm[:], 0.0)
+        nc.scalar.activation(warm[:], warm[:], ACT.Exp)
+        penalty = held.tile([P, C], F32, name="penalty")
         nc.vector.memset(penalty[:], 0.0)
         nc.gpsimd.affine_select(
             out=penalty[:],
             in_=penalty[:],
-            pattern=[[0, SAMPLE_BLOCKS], [1, R], [-1, R]],
+            pattern=[[1, R], [-1, R]],
             compare_op=ALU.not_equal,
             fill=-DIAG_PENALTY,
             base=0,
@@ -60,80 +72,70 @@ def tile_inferencemodel_kernel(tc, latent, edges, query, offs, out):
         )
         identity = held.tile([P, P], BF16, name="identity")
         make_identity(nc, identity[:])
+        minus_two = held.tile([P, PIECE], BF16, name="minus_two")
+        nc.vector.memset(minus_two[:], -2.0)
 
-        groups = SAMPLE_BLOCKS * R
-
-        def grouped(tile_ap):
-            return tile_ap.rearrange("p (g k) -> p g k", k=R)
-
-        def per_group(tile_ap):
-            return tile_ap.unsqueeze(2).to_broadcast([P, groups, R])
-
-        cost = held.tile([P, SAMPLE_BLOCKS * C], F32, name="cost")
-        nc.vector.scalar_tensor_tensor(
-            out=cost[:], in0=lat[:], scalar=-ENTROPY_REG, in1=penalty[:], op0=ALU.mult, op1=ALU.add
-        )
-        top = held.tile([P, groups], F32, name="top")
-        nc.vector.tensor_reduce(out=top[:], in_=grouped(cost[:]), axis=AXIS.X, op=ALU.max)
-        shifted = held.tile([P, SAMPLE_BLOCKS * C], F32, name="shifted")
-        nc.vector.tensor_tensor(grouped(shifted[:]), grouped(cost[:]), per_group(top[:]), ALU.subtract)
-        expd = held.tile([P, SAMPLE_BLOCKS * C], F32, name="expd")
-        nc.scalar.activation(expd[:], shifted[:], ACT.Exp)
-        total = held.tile([P, groups], F32, name="total")
-        nc.vector.tensor_reduce(out=total[:], in_=grouped(expd[:]), axis=AXIS.X, op=ALU.add)
-        inverse = held.tile([P, groups], F32, name="inverse")
-        nc.vector.reciprocal(inverse[:], total[:])
-        twice_adj = held.tile([P, SAMPLE_BLOCKS * C], BF16, name="twice_adj")
-        nc.vector.scalar_tensor_tensor(
-            out=grouped(twice_adj[:]),
-            in0=grouped(expd[:]),
-            scalar=2.0,
-            in1=per_group(inverse[:]),
-            op0=ALU.mult,
-            op1=ALU.mult,
-        )
-
-        flipped = flip.tile([P, PAIR_BLOCKS * SAMPLE_BLOCKS * P], BF16, name="flipped")
-        for cb in range(PAIR_BLOCKS):
-            for h in range(SAMPLE_BLOCKS):
-                block = cb * SAMPLE_BLOCKS + h
-                nc.tensor.transpose(
-                    flipped[:, block * P : (block + 1) * P],
-                    twice_adj[:, h * C + cb * P : h * C + (cb + 1) * P],
-                    identity[:],
-                )
-        weights = held.tile([P, PAIR_BLOCKS * SAMPLE_BLOCKS * P], F32, name="weights")
-        nc.vector.tensor_copy(weights[:], flipped[:])
-
-        keep = []
-        for piece in range(PIECES):
-            keep_piece = held.tile([P, SAMPLE_BLOCKS, PIECE], F32, name=f"keep{piece}")
-            nc.vector.tensor_scalar(
-                out=keep_piece[:], in0=asked[piece][:], scalar1=1.0, scalar2=None, op0=ALU.not_equal
+        expd = []
+        for h in range(SAMPLE_BLOCKS):
+            cost = held.tile([P, C], F32, name=f"cost{h}")
+            nc.vector.scalar_tensor_tensor(
+                out=cost[:], in0=lat[h][:], scalar=-ENTROPY_REG, in1=penalty[:], op0=ALU.mult, op1=ALU.add
             )
-            keep.append(keep_piece)
+            top = held.tile([P, R], F32, name=f"top{h}")
+            nc.vector.tensor_reduce(out=top[:], in_=grouped(cost[:]), axis=AXIS.X, op=ALU.max)
+            shifted = held.tile([P, C], F32, name=f"shifted{h}")
+            nc.vector.tensor_tensor(grouped(shifted[:]), grouped(cost[:]), per_row(top[:]), ALU.subtract)
+            expd_h = ring.tile([P, C], F32, name=f"expd{h}", tag="scalar_out")
+            nc.scalar.activation(expd_h[:], shifted[:], ACT.Exp)
+            expd.append(expd_h)
+
+        weights = []
+        for h in range(SAMPLE_BLOCKS):
+            total = held.tile([P, R], F32, name=f"total{h}")
+            nc.vector.tensor_reduce(out=total[:], in_=grouped(expd[h][:]), axis=AXIS.X, op=ALU.add)
+            inverse = held.tile([P, R], F32, name=f"inverse{h}")
+            nc.vector.reciprocal(inverse[:], total[:])
+            twice_adj = held.tile([P, C], BF16, name=f"twice_adj{h}")
+            nc.vector.scalar_tensor_tensor(
+                out=grouped(twice_adj[:]),
+                in0=grouped(expd[h][:]),
+                scalar=2.0,
+                in1=per_row(inverse[:]),
+                op0=ALU.mult,
+                op1=ALU.mult,
+            )
+            flipped = flip.tile([P, C], BF16, name="flipped")
+            for cb in range(PAIR_BLOCKS):
+                nc.tensor.transpose(
+                    flipped[:, cb * P : (cb + 1) * P], twice_adj[:, cb * P : (cb + 1) * P], identity[:]
+                )
+            weights_h = held.tile([P, C], F32, name=f"weights{h}")
+            nc.vector.tensor_copy(weights_h[:], flipped[:])
+            weights.append(weights_h)
 
         for piece in range(PIECES):
             listed = offsets[:, piece * (PIECE // 16) : (piece + 1) * (PIECE // 16)]
-            picked = []
-            for cb in range(PAIR_BLOCKS):
-                columns = held.tile([P, PIECE], F32, name=f"picked{cb}_{piece}")
-                nc.scalar.activation(columns[:], windows[cb][:].indirect(listed), ACT.Copy)
-                picked.append(columns)
-            result = held.tile([P, SAMPLE_BLOCKS, PIECE], F32, name=f"result{piece}")
+            bank = []
             for h in range(SAMPLE_BLOCKS):
-                bank = banks.tile([P, PIECE], F32, name="bank")
-                for cb in range(PAIR_BLOCKS):
-                    block = cb * SAMPLE_BLOCKS + h
+                bank_h = banks.tile([P, PIECE], F32, name=f"bank{h}")
+                nc.tensor.matmul(bank_h[:], identity[:], minus_two[:], start=True, stop=False)
+                bank.append(bank_h)
+            for cb in range(PAIR_BLOCKS):
+                picked = ring.tile([P, PIECE], F32, name="picked", tag="scalar_out")
+                nc.scalar.activation(picked[:], windows[cb][:].indirect(listed), ACT.Copy)
+                for h in range(SAMPLE_BLOCKS):
                     nc.tensor.matmul(
-                        bank[:],
-                        weights[:, block * P : (block + 1) * P],
-                        picked[cb][:],
-                        start=(cb == 0),
+                        bank[h][:],
+                        weights[h][:, cb * P : (cb + 1) * P],
+                        picked[:],
+                        start=False,
                         stop=(cb == PAIR_BLOCKS - 1),
                     )
+            result = held.tile([P, SAMPLE_BLOCKS, PIECE], F32, name=f"result{piece}")
+            for h in range(SAMPLE_BLOCKS):
                 nc.vector.scalar_tensor_tensor(
-                    out=result[:, h, :], in0=bank[:], scalar=-2.0, in1=keep[piece][:, h, :], op0=ALU.add, op1=ALU.mult
+                    out=result[:, h, :], in0=asked[piece][:, h, :], scalar=1.0, in1=bank[h][:],
+                    op0=ALU.not_equal, op1=ALU.mult,
                 )
                 nc.vector.tensor_scalar(
                     out=result[:, h, :], in0=result[:, h, :], scalar1=1.0, scalar2=None, op0=ALU.add

@@ -28,6 +28,10 @@ def per_row(tile_ap):
     return tile_ap.unsqueeze(2).to_broadcast([P, R, R])
 
 
+def high_halves(tile_ap):
+    return tile_ap.bitcast(BF16).rearrange("p (n half) -> p n half", half=2)[:, :, 1]
+
+
 def tile_inferencemodel_kernel(tc, latent, edges, query, offs, out):
     nc = tc.nc
     with (
@@ -109,7 +113,7 @@ def tile_inferencemodel_kernel(tc, latent, edges, query, offs, out):
                 nc.tensor.transpose(
                     flipped[:, cb * P : (cb + 1) * P], twice_adj[:, cb * P : (cb + 1) * P], identity[:]
                 )
-            weights_h = held.tile([P, C], F32, name=f"weights{h}")
+            weights_h = held.tile([P, C], BF16, name=f"weights{h}")
             nc.vector.tensor_copy(weights_h[:], flipped[:])
             weights.append(weights_h)
 
@@ -127,7 +131,7 @@ def tile_inferencemodel_kernel(tc, latent, edges, query, offs, out):
                     nc.tensor.matmul(
                         bank[h][:],
                         weights[h][:, cb * P : (cb + 1) * P],
-                        picked[:],
+                        high_halves(picked[:]),
                         start=False,
                         stop=(cb == PAIR_BLOCKS - 1),
                     )

@@ -12,8 +12,9 @@ P = 128
 B, R, C, S, N = 256, 16, 256, 2048, 2048
 SAMPLE_BLOCKS = B // P
 PAIR_BLOCKS = C // P
-PIECE = 512
-PIECES = N // PIECE
+BANK = 512
+PIECE_WIDTHS = [BANK, BANK, BANK, BANK // 2, BANK // 2]
+assert sum(PIECE_WIDTHS) == N
 ENTROPY_REG = 0.1
 DIAG_PENALTY = 100000.0
 
@@ -36,7 +37,7 @@ def tile_inferencemodel_kernel(tc, latent, edges, query, offs, out):
     nc = tc.nc
     with (
         tc.tile_pool(name="held", bufs=1) as held,
-        tc.tile_pool(name="ring", bufs=2) as ring,
+        tc.tile_pool(name="ring", bufs=4) as ring,
         tc.psum_pool(name="flip", bufs=SAMPLE_BLOCKS) as flip,
         tc.psum_pool(name="banks", bufs=3) as banks,
     ):
@@ -54,10 +55,11 @@ def tile_inferencemodel_kernel(tc, latent, edges, query, offs, out):
             windows.append(window)
         query_view = query.rearrange("(h p) n -> p h n", p=P)
         out_view = out.rearrange("(h p) n -> p h n", p=P)
+        piece_starts = [sum(PIECE_WIDTHS[:piece]) for piece in range(len(PIECE_WIDTHS))]
         asked = []
-        for piece in range(PIECES):
-            asked_piece = held.tile([P, SAMPLE_BLOCKS, PIECE], F32, name=f"asked{piece}")
-            nc.sync.dma_start(asked_piece[:], query_view[:, :, piece * PIECE : (piece + 1) * PIECE])
+        for piece, (first, width) in enumerate(zip(piece_starts, PIECE_WIDTHS)):
+            asked_piece = held.tile([P, SAMPLE_BLOCKS, width], F32, name=f"asked{piece}")
+            nc.sync.dma_start(asked_piece[:], query_view[:, :, first : first + width])
             asked.append(asked_piece)
 
         warm = held.tile([P, 1], F32, name="warm")
@@ -76,7 +78,7 @@ def tile_inferencemodel_kernel(tc, latent, edges, query, offs, out):
         )
         identity = held.tile([P, P], BF16, name="identity")
         make_identity(nc, identity[:])
-        minus_two = held.tile([P, PIECE], BF16, name="minus_two")
+        minus_two = held.tile([P, BANK], BF16, name="minus_two")
         nc.vector.memset(minus_two[:], -2.0)
 
         expd = []
@@ -87,9 +89,9 @@ def tile_inferencemodel_kernel(tc, latent, edges, query, offs, out):
             )
             top = held.tile([P, R], F32, name=f"top{h}")
             nc.vector.tensor_reduce(out=top[:], in_=grouped(cost[:]), axis=AXIS.X, op=ALU.max)
-            shifted = held.tile([P, C], F32, name=f"shifted{h}")
+            shifted = ring.tile([P, C], F32, name=f"shifted{h}", tag="scalar_ring")
             nc.vector.tensor_tensor(grouped(shifted[:]), grouped(cost[:]), per_row(top[:]), ALU.subtract)
-            expd_h = ring.tile([P, C], F32, name=f"expd{h}", tag="scalar_out")
+            expd_h = ring.tile([P, C], F32, name=f"expd{h}", tag="scalar_ring")
             nc.scalar.activation(expd_h[:], shifted[:], ACT.Exp)
             expd.append(expd_h)
 
@@ -117,15 +119,15 @@ def tile_inferencemodel_kernel(tc, latent, edges, query, offs, out):
             nc.vector.tensor_copy(weights_h[:], flipped[:])
             weights.append(weights_h)
 
-        for piece in range(PIECES):
-            listed = offsets[:, piece * (PIECE // 16) : (piece + 1) * (PIECE // 16)]
+        for piece, (first, width) in enumerate(zip(piece_starts, PIECE_WIDTHS)):
+            listed = offsets[:, first // 16 : (first + width) // 16]
             bank = []
             for h in range(SAMPLE_BLOCKS):
-                bank_h = banks.tile([P, PIECE], F32, name=f"bank{h}")
-                nc.tensor.matmul(bank_h[:], identity[:], minus_two[:], start=True, stop=False)
+                bank_h = banks.tile([P, width], F32, name=f"bank{h}")
+                nc.tensor.matmul(bank_h[:], identity[:], minus_two[:, :width], start=True, stop=False)
                 bank.append(bank_h)
             for cb in range(PAIR_BLOCKS):
-                picked = ring.tile([P, PIECE], F32, name="picked", tag="scalar_out")
+                picked = ring.tile([P, width], F32, name="picked", tag="scalar_ring")
                 nc.scalar.activation(picked[:], windows[cb][:].indirect(listed), ACT.Copy)
                 for h in range(SAMPLE_BLOCKS):
                     nc.tensor.matmul(
@@ -135,7 +137,7 @@ def tile_inferencemodel_kernel(tc, latent, edges, query, offs, out):
                         start=False,
                         stop=(cb == PAIR_BLOCKS - 1),
                     )
-            result = held.tile([P, SAMPLE_BLOCKS, PIECE], F32, name=f"result{piece}")
+            result = held.tile([P, SAMPLE_BLOCKS, width], F32, name=f"result{piece}")
             for h in range(SAMPLE_BLOCKS):
                 nc.vector.scalar_tensor_tensor(
                     out=result[:, h, :], in0=asked[piece][:, h, :], scalar=1.0, in1=bank[h][:],
@@ -144,4 +146,4 @@ def tile_inferencemodel_kernel(tc, latent, edges, query, offs, out):
                 nc.vector.tensor_scalar(
                     out=result[:, h, :], in0=result[:, h, :], scalar1=1.0, scalar2=None, op0=ALU.add
                 )
-            nc.sync.dma_start(out_view[:, :, piece * PIECE : (piece + 1) * PIECE], result[:])
+            nc.sync.dma_start(out_view[:, :, first : first + width], result[:])

@@ -119,31 +119,40 @@ def tile_inferencemodel_kernel(tc, latent, edges, query, offs, out):
             nc.vector.tensor_copy(weights_h[:], flipped[:])
             weights.append(weights_h)
 
-        for piece, (first, width) in enumerate(zip(piece_starts, PIECE_WIDTHS)):
-            listed = offsets[:, first // 16 : (first + width) // 16]
-            bank = []
-            for h in range(SAMPLE_BLOCKS):
-                bank_h = banks.tile([P, width], F32, name=f"bank{h}")
-                nc.tensor.matmul(bank_h[:], identity[:], minus_two[:, :width], start=True, stop=False)
-                bank.append(bank_h)
-            for cb in range(PAIR_BLOCKS):
-                picked = ring.tile([P, width], F32, name="picked", tag="scalar_ring")
-                nc.scalar.activation(picked[:], windows[cb][:].indirect(listed), ACT.Copy)
+        turns = []
+        for step in range(len(PIECE_WIDTHS) + 1):
+            if step < len(PIECE_WIDTHS):
+                turns.append((step, 0))
+            if step > 0:
+                turns.append((step - 1, 1))
+        bank = {}
+        for piece, cb in turns:
+            first, width = piece_starts[piece], PIECE_WIDTHS[piece]
+            if cb == 0:
+                bank[piece] = []
                 for h in range(SAMPLE_BLOCKS):
-                    nc.tensor.matmul(
-                        bank[h][:],
-                        weights[h][:, cb * P : (cb + 1) * P],
-                        high_halves(picked[:]),
-                        start=False,
-                        stop=(cb == PAIR_BLOCKS - 1),
-                    )
-            result = held.tile([P, SAMPLE_BLOCKS, width], F32, name=f"result{piece}")
+                    bank_h = banks.tile([P, width], F32, name=f"bank{h}")
+                    nc.tensor.matmul(bank_h[:], identity[:], minus_two[:, :width], start=True, stop=False)
+                    bank[piece].append(bank_h)
+            picked = ring.tile([P, width], F32, name="picked", tag="scalar_ring")
+            listed = offsets[:, first // 16 : (first + width) // 16]
+            nc.scalar.activation(picked[:], windows[cb][:].indirect(listed), ACT.Copy)
             for h in range(SAMPLE_BLOCKS):
-                nc.vector.scalar_tensor_tensor(
-                    out=result[:, h, :], in0=asked[piece][:, h, :], scalar=1.0, in1=bank[h][:],
-                    op0=ALU.not_equal, op1=ALU.mult,
+                nc.tensor.matmul(
+                    bank[piece][h][:],
+                    weights[h][:, cb * P : (cb + 1) * P],
+                    high_halves(picked[:]),
+                    start=False,
+                    stop=(cb == PAIR_BLOCKS - 1),
                 )
-                nc.vector.tensor_scalar(
-                    out=result[:, h, :], in0=result[:, h, :], scalar1=1.0, scalar2=None, op0=ALU.add
-                )
-            nc.sync.dma_start(out_view[:, :, first : first + width], result[:])
+            if cb == PAIR_BLOCKS - 1:
+                result = held.tile([P, SAMPLE_BLOCKS, width], F32, name=f"result{piece}")
+                for h in range(SAMPLE_BLOCKS):
+                    nc.vector.scalar_tensor_tensor(
+                        out=result[:, h, :], in0=asked[piece][:, h, :], scalar=1.0, in1=bank[piece][h][:],
+                        op0=ALU.not_equal, op1=ALU.mult,
+                    )
+                    nc.vector.tensor_scalar(
+                        out=result[:, h, :], in0=result[:, h, :], scalar1=1.0, scalar2=None, op0=ALU.add
+                    )
+                nc.sync.dma_start(out_view[:, :, first : first + width], result[:])

@@ -17,6 +17,7 @@ PIECE_WIDTHS = [BANK, BANK, BANK, BANK // 2, BANK // 2]
 assert sum(PIECE_WIDTHS) == N
 ENTROPY_REG = 0.1
 DIAG_PENALTY = 100000.0
+PUSH = 8.0
 
 FLOPS = 2 * B * C * N
 
@@ -78,8 +79,8 @@ def tile_inferencemodel_kernel(tc, latent, edges, query, offs, out):
         )
         identity = held.tile([P, P], BF16, name="identity")
         make_identity(nc, identity[:])
-        minus_two = held.tile([P, BANK], BF16, name="minus_two")
-        nc.vector.memset(minus_two[:], -2.0)
+        pusher = held.tile([P, P], BF16, name="pusher")
+        nc.vector.tensor_scalar(out=pusher[:], in0=identity[:], scalar1=-PUSH, scalar2=None, op0=ALU.mult)
 
         expd = []
         for h in range(SAMPLE_BLOCKS):
@@ -132,7 +133,9 @@ def tile_inferencemodel_kernel(tc, latent, edges, query, offs, out):
                 bank[piece] = []
                 for h in range(SAMPLE_BLOCKS):
                     bank_h = banks.tile([P, width], F32, name=f"bank{h}")
-                    nc.tensor.matmul(bank_h[:], identity[:], minus_two[:, :width], start=True, stop=False)
+                    nc.tensor.matmul(
+                        bank_h[:], pusher[:], high_halves(asked[piece][:, h, :]), start=True, stop=False
+                    )
                     bank[piece].append(bank_h)
             picked = ring.tile([P, width], F32, name="picked", tag="scalar_ring")
             listed = offsets[:, first // 16 : (first + width) // 16]
@@ -149,10 +152,7 @@ def tile_inferencemodel_kernel(tc, latent, edges, query, offs, out):
                 result = held.tile([P, SAMPLE_BLOCKS, width], F32, name=f"result{piece}")
                 for h in range(SAMPLE_BLOCKS):
                     nc.vector.scalar_tensor_tensor(
-                        out=result[:, h, :], in0=asked[piece][:, h, :], scalar=1.0, in1=bank[piece][h][:],
-                        op0=ALU.not_equal, op1=ALU.mult,
-                    )
-                    nc.vector.tensor_scalar(
-                        out=result[:, h, :], in0=result[:, h, :], scalar1=1.0, scalar2=None, op0=ALU.add
+                        out=result[:, h, :], in0=bank[piece][h][:], scalar=-(PUSH + 1.0), in1=asked[piece][:, h, :],
+                        op0=ALU.add, op1=ALU.max,
                     )
                 nc.sync.dma_start(out_view[:, :, first : first + width], result[:])

@@ -130,13 +130,12 @@ def tile_inferencemodel_kernel(tc, latent, edges, query, offs, out):
         for piece, cb in turns:
             first, width = piece_starts[piece], PIECE_WIDTHS[piece]
             if cb == 0:
-                bank[piece] = []
+                bank[piece] = [banks.tile([P, width], F32, name=f"bank{h}") for h in range(SAMPLE_BLOCKS)]
+            else:
                 for h in range(SAMPLE_BLOCKS):
-                    bank_h = banks.tile([P, width], F32, name=f"bank{h}")
                     nc.tensor.matmul(
-                        bank_h[:], pusher[:], high_halves(asked[piece][:, h, :]), start=True, stop=False
+                        bank[piece][h][:], pusher[:], high_halves(asked[piece][:, h, :]), start=False, stop=False
                     )
-                    bank[piece].append(bank_h)
             picked = ring.tile([P, width], F32, name="picked", tag="scalar_ring")
             listed = offsets[:, first // 16 : (first + width) // 16]
             nc.scalar.activation(picked[:], windows[cb][:].indirect(listed), ACT.Copy)
@@ -145,7 +144,7 @@ def tile_inferencemodel_kernel(tc, latent, edges, query, offs, out):
                     bank[piece][h][:],
                     weights[h][:, cb * P : (cb + 1) * P],
                     high_halves(picked[:]),
-                    start=False,
+                    start=(cb == 0),
                     stop=(cb == PAIR_BLOCKS - 1),
                 )
             if cb == PAIR_BLOCKS - 1:

@@ -15,6 +15,8 @@ PAIR_BLOCKS = C // P
 BANK = 512
 PIECE_WIDTHS = [BANK, BANK, BANK, BANK // 2, BANK // 2]
 assert sum(PIECE_WIDTHS) == N
+EARLY = 2
+CHUNK = 512
 ENTROPY_REG = 0.1
 DIAG_PENALTY = 100000.0
 PUSH = 8.0
@@ -30,8 +32,16 @@ def per_row(tile_ap):
     return tile_ap.unsqueeze(2).to_broadcast([P, R, R])
 
 
+def halves(tile_ap):
+    return tile_ap.bitcast(BF16).rearrange("p (n half) -> p n half", half=2)
+
+
+def low_halves(tile_ap):
+    return halves(tile_ap)[:, :, 0]
+
+
 def high_halves(tile_ap):
-    return tile_ap.bitcast(BF16).rearrange("p (n half) -> p n half", half=2)[:, :, 1]
+    return halves(tile_ap)[:, :, 1]
 
 
 def tile_inferencemodel_kernel(tc, latent, edges, query, offs, out):
@@ -120,38 +130,62 @@ def tile_inferencemodel_kernel(tc, latent, edges, query, offs, out):
             nc.vector.tensor_copy(weights_h[:], flipped[:])
             weights.append(weights_h)
 
-        turns = []
-        for step in range(len(PIECE_WIDTHS) + 1):
-            if step < len(PIECE_WIDTHS):
-                turns.append((step, 0))
-            if step > 0:
-                turns.append((step - 1, 1))
         bank = {}
-        for piece, cb in turns:
+
+        def open_banks(piece):
+            width = PIECE_WIDTHS[piece]
+            bank[piece] = [banks.tile([P, width], F32, name=f"bank{h}") for h in range(SAMPLE_BLOCKS)]
+
+        def look_up(window, piece):
             first, width = piece_starts[piece], PIECE_WIDTHS[piece]
-            if cb == 0:
-                bank[piece] = [banks.tile([P, width], F32, name=f"bank{h}") for h in range(SAMPLE_BLOCKS)]
-            else:
-                for h in range(SAMPLE_BLOCKS):
-                    nc.tensor.matmul(
-                        bank[piece][h][:], pusher[:], high_halves(asked[piece][:, h, :]), start=False, stop=False
-                    )
             picked = ring.tile([P, width], F32, name="picked", tag="scalar_ring")
             listed = offsets[:, first // 16 : (first + width) // 16]
-            nc.scalar.activation(picked[:], windows[cb][:].indirect(listed), ACT.Copy)
+            nc.scalar.activation(picked[:], window[:].indirect(listed), ACT.Copy)
+            return picked
+
+        def multiply(piece, cb, picked_columns):
             for h in range(SAMPLE_BLOCKS):
                 nc.tensor.matmul(
                     bank[piece][h][:],
                     weights[h][:, cb * P : (cb + 1) * P],
-                    high_halves(picked[:]),
+                    picked_columns,
                     start=(cb == 0),
                     stop=(cb == PAIR_BLOCKS - 1),
                 )
-            if cb == PAIR_BLOCKS - 1:
-                result = held.tile([P, SAMPLE_BLOCKS, width], F32, name=f"result{piece}")
-                for h in range(SAMPLE_BLOCKS):
-                    nc.vector.scalar_tensor_tensor(
-                        out=result[:, h, :], in0=bank[piece][h][:], scalar=-(PUSH + 1.0), in1=asked[piece][:, h, :],
-                        op0=ALU.add, op1=ALU.max,
-                    )
-                nc.sync.dma_start(out_view[:, :, first : first + width], result[:])
+
+        def push(piece):
+            for h in range(SAMPLE_BLOCKS):
+                nc.tensor.matmul(
+                    bank[piece][h][:], pusher[:], high_halves(asked[piece][:, h, :]), start=False, stop=False
+                )
+
+        def paint_and_store(piece):
+            first, width = piece_starts[piece], PIECE_WIDTHS[piece]
+            result = held.tile([P, SAMPLE_BLOCKS, width], F32, name=f"result{piece}")
+            for h in range(SAMPLE_BLOCKS):
+                nc.vector.scalar_tensor_tensor(
+                    out=result[:, h, :], in0=bank[piece][h][:], scalar=-(PUSH + 1.0), in1=asked[piece][:, h, :],
+                    op0=ALU.add, op1=ALU.max,
+                )
+            nc.sync.dma_start(out_view[:, :, first : first + width], result[:])
+
+        for piece in range(EARLY):
+            open_banks(piece)
+            picked = look_up(windows[0], piece)
+            multiply(piece, 0, high_halves(picked[:]))
+        for first in range(0, S, CHUNK):
+            nc.vector.tensor_copy(
+                low_halves(windows[0][:, first : first + CHUNK]), windows[1][:, first : first + CHUNK]
+            )
+        for piece in range(EARLY):
+            push(piece)
+            picked = look_up(windows[1], piece)
+            multiply(piece, 1, high_halves(picked[:]))
+            paint_and_store(piece)
+        for piece in range(EARLY, len(PIECE_WIDTHS)):
+            open_banks(piece)
+            picked = look_up(windows[0], piece)
+            multiply(piece, 0, high_halves(picked[:]))
+            push(piece)
+            multiply(piece, 1, low_halves(picked[:]))
+            paint_and_store(piece)

@@ -131,10 +131,12 @@ def tile_inferencemodel_kernel(tc, latent, edges, query, offs, out):
             weights.append(weights_h)
 
         bank = {}
+        result = {}
 
         def open_banks(piece):
             width = PIECE_WIDTHS[piece]
             bank[piece] = [banks.tile([P, width], F32, name=f"bank{h}") for h in range(SAMPLE_BLOCKS)]
+            result[piece] = held.tile([P, SAMPLE_BLOCKS, width], F32, name=f"result{piece}")
 
         def look_up(window, piece):
             first, width = piece_starts[piece], PIECE_WIDTHS[piece]
@@ -143,49 +145,53 @@ def tile_inferencemodel_kernel(tc, latent, edges, query, offs, out):
             nc.scalar.activation(picked[:], window[:].indirect(listed), ACT.Copy)
             return picked
 
-        def multiply(piece, cb, picked_columns):
-            for h in range(SAMPLE_BLOCKS):
-                nc.tensor.matmul(
-                    bank[piece][h][:],
-                    weights[h][:, cb * P : (cb + 1) * P],
-                    picked_columns,
-                    start=(cb == 0),
-                    stop=(cb == PAIR_BLOCKS - 1),
-                )
+        def multiply(piece, h, cb, picked_columns):
+            nc.tensor.matmul(
+                bank[piece][h][:],
+                weights[h][:, cb * P : (cb + 1) * P],
+                picked_columns,
+                start=(cb == 0),
+                stop=(cb == PAIR_BLOCKS - 1),
+            )
 
-        def push(piece):
-            for h in range(SAMPLE_BLOCKS):
-                nc.tensor.matmul(
-                    bank[piece][h][:], pusher[:], high_halves(asked[piece][:, h, :]), start=False, stop=False
-                )
+        def push(piece, h):
+            nc.tensor.matmul(
+                bank[piece][h][:], pusher[:], high_halves(asked[piece][:, h, :]), start=False, stop=False
+            )
 
-        def paint_and_store(piece):
+        def paint(piece, h):
+            nc.vector.scalar_tensor_tensor(
+                out=result[piece][:, h, :], in0=bank[piece][h][:], scalar=-(PUSH + 1.0), in1=asked[piece][:, h, :],
+                op0=ALU.add, op1=ALU.max,
+            )
+
+        def store(piece, h):
             first, width = piece_starts[piece], PIECE_WIDTHS[piece]
-            result = held.tile([P, SAMPLE_BLOCKS, width], F32, name=f"result{piece}")
-            for h in range(SAMPLE_BLOCKS):
-                nc.vector.scalar_tensor_tensor(
-                    out=result[:, h, :], in0=bank[piece][h][:], scalar=-(PUSH + 1.0), in1=asked[piece][:, h, :],
-                    op0=ALU.add, op1=ALU.max,
-                )
-            nc.sync.dma_start(out_view[:, :, first : first + width], result[:])
+            nc.sync.dma_start(out_view[:, h, first : first + width], result[piece][:, h, :])
 
         for piece in range(EARLY):
             open_banks(piece)
             picked = look_up(windows[0], piece)
-            multiply(piece, 0, high_halves(picked[:]))
+            for h in range(SAMPLE_BLOCKS):
+                multiply(piece, h, 0, high_halves(picked[:]))
         for first in range(0, S, CHUNK):
             nc.vector.tensor_copy(
                 low_halves(windows[0][:, first : first + CHUNK]), windows[1][:, first : first + CHUNK]
             )
         for piece in range(EARLY):
-            push(piece)
+            for h in range(SAMPLE_BLOCKS):
+                push(piece, h)
             picked = look_up(windows[1], piece)
-            multiply(piece, 1, high_halves(picked[:]))
-            paint_and_store(piece)
+            for h in range(SAMPLE_BLOCKS):
+                multiply(piece, h, 1, high_halves(picked[:]))
+                paint(piece, h)
+                store(piece, h)
         for piece in range(EARLY, len(PIECE_WIDTHS)):
             open_banks(piece)
             picked = look_up(windows[0], piece)
-            multiply(piece, 0, high_halves(picked[:]))
-            push(piece)
-            multiply(piece, 1, low_halves(picked[:]))
-            paint_and_store(piece)
+            for h in range(SAMPLE_BLOCKS):
+                multiply(piece, h, 0, high_halves(picked[:]))
+                push(piece, h)
+                multiply(piece, h, 1, low_halves(picked[:]))
+                paint(piece, h)
+                store(piece, h)

@@ -147,16 +147,12 @@ def tile_inferencemodel_kernel(tc, latent, edges, query, offs, out):
 
         def multiply(piece, h, cb, picked_columns):
             nc.tensor.matmul(
-                bank[piece][h][:],
-                weights[h][:, cb * P : (cb + 1) * P],
-                picked_columns,
-                start=(cb == 0),
-                stop=(cb == PAIR_BLOCKS - 1),
+                bank[piece][h][:], weights[h][:, cb * P : (cb + 1) * P], picked_columns, start=(cb == 0), stop=False
             )
 
         def push(piece, h):
             nc.tensor.matmul(
-                bank[piece][h][:], pusher[:], high_halves(asked[piece][:, h, :]), start=False, stop=False
+                bank[piece][h][:], pusher[:], high_halves(asked[piece][:, h, :]), start=False, stop=True
             )
 
         def paint(piece, h):
@@ -179,11 +175,10 @@ def tile_inferencemodel_kernel(tc, latent, edges, query, offs, out):
                 low_halves(windows[0][:, first : first + CHUNK]), windows[1][:, first : first + CHUNK]
             )
         for piece in range(EARLY):
-            for h in range(SAMPLE_BLOCKS):
-                push(piece, h)
             picked = look_up(windows[1], piece)
             for h in range(SAMPLE_BLOCKS):
                 multiply(piece, h, 1, high_halves(picked[:]))
+                push(piece, h)
                 paint(piece, h)
                 store(piece, h)
         for piece in range(EARLY, len(PIECE_WIDTHS)):
@@ -191,7 +186,7 @@ def tile_inferencemodel_kernel(tc, latent, edges, query, offs, out):
             picked = look_up(windows[0], piece)
             for h in range(SAMPLE_BLOCKS):
                 multiply(piece, h, 0, high_halves(picked[:]))
-                push(piece, h)
                 multiply(piece, h, 1, low_halves(picked[:]))
+                push(piece, h)
                 paint(piece, h)
                 store(piece, h)

@@ -17,6 +17,7 @@ PIECE_WIDTHS = [BANK, BANK, BANK, BANK // 2, BANK // 2]
 assert sum(PIECE_WIDTHS) == N
 EARLY = 2
 CHUNK = 512
+PLACES = 3
 ENTROPY_REG = 0.1
 DIAG_PENALTY = 100000.0
 PUSH = 8.0
@@ -48,7 +49,6 @@ def tile_inferencemodel_kernel(tc, latent, edges, query, offs, out):
     nc = tc.nc
     with (
         tc.tile_pool(name="held", bufs=1) as held,
-        tc.tile_pool(name="ring", bufs=4) as ring,
         tc.psum_pool(name="flip", bufs=SAMPLE_BLOCKS) as flip,
         tc.psum_pool(name="banks", bufs=3) as banks,
     ):
@@ -92,6 +92,7 @@ def tile_inferencemodel_kernel(tc, latent, edges, query, offs, out):
         pusher = held.tile([P, P], BF16, name="pusher")
         nc.vector.tensor_scalar(out=pusher[:], in0=identity[:], scalar1=-PUSH, scalar2=None, op0=ALU.mult)
 
+        first_holder = {"shifted1": "place0", "expd0": "place1", "expd1": "place2"}
         expd = []
         for h in range(SAMPLE_BLOCKS):
             cost = held.tile([P, C], F32, name=f"cost{h}")
@@ -100,9 +101,9 @@ def tile_inferencemodel_kernel(tc, latent, edges, query, offs, out):
             )
             top = held.tile([P, R], F32, name=f"top{h}")
             nc.vector.tensor_reduce(out=top[:], in_=grouped(cost[:]), axis=AXIS.X, op=ALU.max)
-            shifted = ring.tile([P, C], F32, name=f"shifted{h}", tag="scalar_ring")
+            shifted = held.tile([P, C], F32, name=f"shifted{h}", tag=first_holder.get(f"shifted{h}", f"shifted{h}"))
             nc.vector.tensor_tensor(grouped(shifted[:]), grouped(cost[:]), per_row(top[:]), ALU.subtract)
-            expd_h = ring.tile([P, C], F32, name=f"expd{h}", tag="scalar_ring")
+            expd_h = held.tile([P, C], F32, name=f"expd{h}", tag=first_holder[f"expd{h}"])
             nc.scalar.activation(expd_h[:], shifted[:], ACT.Exp)
             expd.append(expd_h)
 
@@ -132,6 +133,7 @@ def tile_inferencemodel_kernel(tc, latent, edges, query, offs, out):
 
         bank = {}
         result = {}
+        picked_tiles = []
 
         def open_banks(piece):
             width = PIECE_WIDTHS[piece]
@@ -140,7 +142,9 @@ def tile_inferencemodel_kernel(tc, latent, edges, query, offs, out):
 
         def look_up(window, piece):
             first, width = piece_starts[piece], PIECE_WIDTHS[piece]
-            picked = ring.tile([P, width], F32, name="picked", tag="scalar_ring")
+            turn = len(picked_tiles)
+            picked = held.tile([P, width], F32, name=f"picked{turn}", tag=f"place{turn % PLACES}")
+            picked_tiles.append(picked)
             listed = offsets[:, first // 16 : (first + width) // 16]
             nc.scalar.activation(picked[:], window[:].indirect(listed), ACT.Copy)
             return picked

@@ -13,7 +13,7 @@ B, R, C, S, N = 256, 16, 256, 2048, 2048
 SAMPLE_BLOCKS = B // P
 PAIR_BLOCKS = C // P
 BANK = 512
-PIECE_WIDTHS = [BANK, BANK, BANK, BANK // 2, BANK // 2]
+PIECE_WIDTHS = [BANK, BANK, BANK // 2, BANK // 2, BANK // 2, BANK // 2]
 assert sum(PIECE_WIDTHS) == N
 EARLY = 2
 CHUNK = 512

@@ -13,7 +13,7 @@ B, R, C, S, N = 256, 16, 256, 2048, 2048
 SAMPLE_BLOCKS = B // P
 PAIR_BLOCKS = C // P
 BANK = 512
-PIECE_WIDTHS = [BANK, BANK, BANK // 2, BANK // 2, BANK // 2, BANK // 2]
+PIECE_WIDTHS = [BANK, 3 * BANK // 4, BANK // 2, 3 * BANK // 4, BANK // 2, BANK // 2]
 assert sum(PIECE_WIDTHS) == N
 EARLY = 2
 CHUNK = 512

@@ -13,7 +13,7 @@ B, R, C, S, N = 256, 16, 256, 2048, 2048
 SAMPLE_BLOCKS = B // P
 PAIR_BLOCKS = C // P
 BANK = 512
-PIECE_WIDTHS = [BANK, 3 * BANK // 4, BANK // 2, 3 * BANK // 4, BANK // 2, BANK // 2]
+PIECE_WIDTHS = [BANK, 5 * BANK // 8, BANK // 2, 7 * BANK // 8, BANK // 2, BANK // 2]
 assert sum(PIECE_WIDTHS) == N
 EARLY = 2
 CHUNK = 512

@@ -16,7 +16,6 @@ BANK = 512
 PIECE_WIDTHS = [BANK, 5 * BANK // 8, BANK // 2, 7 * BANK // 8, BANK // 2, BANK // 2]
 assert sum(PIECE_WIDTHS) == N
 EARLY = 2
-CHUNK = 512
 PLACES = 3
 ENTROPY_REG = 0.1
 DIAG_PENALTY = 100000.0
@@ -174,10 +173,7 @@ def tile_inferencemodel_kernel(tc, latent, edges, query, offs, out):
             picked = look_up(windows[0], piece)
             for h in range(SAMPLE_BLOCKS):
                 multiply(piece, h, 0, high_halves(picked[:]))
-        for first in range(0, S, CHUNK):
-            nc.vector.tensor_copy(
-                low_halves(windows[0][:, first : first + CHUNK]), windows[1][:, first : first + CHUNK]
-            )
+        nc.vector.tensor_copy(low_halves(windows[0][:]), windows[1][:])
         for piece in range(EARLY):
             picked = look_up(windows[1], piece)
             for h in range(SAMPLE_BLOCKS):

import concourse.mybir as mybir
from concourse.masks import make_identity

F32 = mybir.dt.float32
BF16 = mybir.dt.bfloat16
U16 = mybir.dt.uint16
ALU = mybir.AluOpType
ACT = mybir.ActivationFunctionType
AXIS = mybir.AxisListType

P = 128
B, R, C, S, N = 256, 16, 256, 2048, 2048
SAMPLE_BLOCKS = B // P
PAIR_BLOCKS = C // P
BANK = 512
PIECE_WIDTHS = [BANK, 5 * BANK // 8, BANK // 2, 7 * BANK // 8, BANK // 2, BANK // 2]
assert sum(PIECE_WIDTHS) == N
EARLY = 2
PLACES = 3
ENTROPY_REG = 0.1
DIAG_PENALTY = 100000.0
PUSH = 8.0

FLOPS = 2 * B * C * N


def grouped(tile_ap):
    return tile_ap.rearrange("p (i k) -> p i k", k=R)


def per_row(tile_ap):
    return tile_ap.unsqueeze(2).to_broadcast([P, R, R])


def halves(tile_ap):
    return tile_ap.bitcast(BF16).rearrange("p (n half) -> p n half", half=2)


def low_halves(tile_ap):
    return halves(tile_ap)[:, :, 0]


def high_halves(tile_ap):
    return halves(tile_ap)[:, :, 1]


def tile_inferencemodel_kernel(tc, latent, edges, query, offs, out):
    nc = tc.nc
    with (
        tc.tile_pool(name="held", bufs=1) as held,
        tc.psum_pool(name="flip", bufs=SAMPLE_BLOCKS) as flip,
        tc.psum_pool(name="banks", bufs=3) as banks,
    ):
        lat = []
        for h in range(SAMPLE_BLOCKS):
            lat_h = held.tile([P, C], F32, name=f"lat{h}")
            nc.sync.dma_start(lat_h[:], latent[h * P : (h + 1) * P, :])
            lat.append(lat_h)
        offsets = held.tile([P, N // 16], U16, name="offsets")
        nc.sync.dma_start(offsets[:], offs)
        windows = []
        for cb in range(PAIR_BLOCKS):
            window = held.tile([P, S], F32, name=f"window{cb}")
            nc.sync.dma_start(window[:], edges[cb * P : (cb + 1) * P, :])
            windows.append(window)
        query_view = query.rearrange("(h p) n -> p h n", p=P)
        out_view = out.rearrange("(h p) n -> p h n", p=P)
        piece_starts = [sum(PIECE_WIDTHS[:piece]) for piece in range(len(PIECE_WIDTHS))]
        asked = []
        for piece, (first, width) in enumerate(zip(piece_starts, PIECE_WIDTHS)):
            asked_piece = held.tile([P, SAMPLE_BLOCKS, width], F32, name=f"asked{piece}")
            nc.sync.dma_start(asked_piece[:], query_view[:, :, first : first + width])
            asked.append(asked_piece)

        warm = held.tile([P, 1], F32, name="warm")
        nc.vector.memset(warm[:], 0.0)
        nc.scalar.activation(warm[:], warm[:], ACT.Exp)
        penalty = held.tile([P, C], F32, name="penalty")
        nc.vector.memset(penalty[:], 0.0)
        nc.gpsimd.affine_select(
            out=penalty[:],
            in_=penalty[:],
            pattern=[[1, R], [-1, R]],
            compare_op=ALU.not_equal,
            fill=-DIAG_PENALTY,
            base=0,
            channel_multiplier=0,
        )
        identity = held.tile([P, P], BF16, name="identity")
        make_identity(nc, identity[:])
        pusher = held.tile([P, P], BF16, name="pusher")
        nc.vector.tensor_scalar(out=pusher[:], in0=identity[:], scalar1=-PUSH, scalar2=None, op0=ALU.mult)

        first_holder = {"shifted1": "place0", "expd0": "place1", "expd1": "place2"}
        expd = []
        for h in range(SAMPLE_BLOCKS):
            cost = held.tile([P, C], F32, name=f"cost{h}")
            nc.vector.scalar_tensor_tensor(
                out=cost[:], in0=lat[h][:], scalar=-ENTROPY_REG, in1=penalty[:], op0=ALU.mult, op1=ALU.add
            )
            top = held.tile([P, R], F32, name=f"top{h}")
            nc.vector.tensor_reduce(out=top[:], in_=grouped(cost[:]), axis=AXIS.X, op=ALU.max)
            shifted = held.tile([P, C], F32, name=f"shifted{h}", tag=first_holder.get(f"shifted{h}", f"shifted{h}"))
            nc.vector.tensor_tensor(grouped(shifted[:]), grouped(cost[:]), per_row(top[:]), ALU.subtract)
            expd_h = held.tile([P, C], F32, name=f"expd{h}", tag=first_holder[f"expd{h}"])
            nc.scalar.activation(expd_h[:], shifted[:], ACT.Exp)
            expd.append(expd_h)

        weights = []
        for h in range(SAMPLE_BLOCKS):
            total = held.tile([P, R], F32, name=f"total{h}")
            nc.vector.tensor_reduce(out=total[:], in_=grouped(expd[h][:]), axis=AXIS.X, op=ALU.add)
            inverse = held.tile([P, R], F32, name=f"inverse{h}")
            nc.vector.reciprocal(inverse[:], total[:])
            twice_adj = held.tile([P, C], BF16, name=f"twice_adj{h}")
            nc.vector.scalar_tensor_tensor(
                out=grouped(twice_adj[:]),
                in0=grouped(expd[h][:]),
                scalar=2.0,
                in1=per_row(inverse[:]),
                op0=ALU.mult,
                op1=ALU.mult,
            )
            flipped = flip.tile([P, C], BF16, name="flipped")
            for cb in range(PAIR_BLOCKS):
                nc.tensor.transpose(
                    flipped[:, cb * P : (cb + 1) * P], twice_adj[:, cb * P : (cb + 1) * P], identity[:]
                )
            weights_h = held.tile([P, C], BF16, name=f"weights{h}")
            nc.vector.tensor_copy(weights_h[:], flipped[:])
            weights.append(weights_h)

        bank = {}
        result = {}
        picked_tiles = []

        def open_banks(piece):
            width = PIECE_WIDTHS[piece]
            bank[piece] = [banks.tile([P, width], F32, name=f"bank{h}") for h in range(SAMPLE_BLOCKS)]
            result[piece] = held.tile([P, SAMPLE_BLOCKS, width], F32, name=f"result{piece}")

        def look_up(window, piece):
            first, width = piece_starts[piece], PIECE_WIDTHS[piece]
            turn = len(picked_tiles)
            picked = held.tile([P, width], F32, name=f"picked{turn}", tag=f"place{turn % PLACES}")
            picked_tiles.append(picked)
            listed = offsets[:, first // 16 : (first + width) // 16]
            nc.scalar.activation(picked[:], window[:].indirect(listed), ACT.Copy)
            return picked

        def multiply(piece, h, cb, picked_columns):
            nc.tensor.matmul(
                bank[piece][h][:], weights[h][:, cb * P : (cb + 1) * P], picked_columns, start=(cb == 0), stop=False
            )

        def push(piece, h):
            nc.tensor.matmul(
                bank[piece][h][:], pusher[:], high_halves(asked[piece][:, h, :]), start=False, stop=True
            )

        def paint(piece, h):
            nc.vector.scalar_tensor_tensor(
                out=result[piece][:, h, :], in0=bank[piece][h][:], scalar=-(PUSH + 1.0), in1=asked[piece][:, h, :],
                op0=ALU.add, op1=ALU.max,
            )

        def store(piece, h):
            first, width = piece_starts[piece], PIECE_WIDTHS[piece]
            nc.sync.dma_start(out_view[:, h, first : first + width], result[piece][:, h, :])

        for piece in range(EARLY):
            open_banks(piece)
            picked = look_up(windows[0], piece)
            for h in range(SAMPLE_BLOCKS):
                multiply(piece, h, 0, high_halves(picked[:]))
        nc.vector.tensor_copy(low_halves(windows[0][:]), windows[1][:])
        for piece in range(EARLY):
            picked = look_up(windows[1], piece)
            for h in range(SAMPLE_BLOCKS):
                multiply(piece, h, 1, high_halves(picked[:]))
                push(piece, h)
                paint(piece, h)
                store(piece, h)
        for piece in range(EARLY, len(PIECE_WIDTHS)):
            open_banks(piece)
            picked = look_up(windows[0], piece)
            for h in range(SAMPLE_BLOCKS):
                multiply(piece, h, 0, high_halves(picked[:]))
                multiply(piece, h, 1, low_halves(picked[:]))
                push(piece, h)
                paint(piece, h)
                store(piece, h)
